import numpy as np
import ml_dtypes


def mxq(x, axis, fmt="e4m3"):
    dtype, down = {"e4m3": (ml_dtypes.float8_e4m3fn, 7), "e5m2": (ml_dtypes.float8_e5m2, 14)}[fmt]
    v = np.moveaxis(np.asarray(x, np.float32).astype(ml_dtypes.bfloat16).astype(np.float64), axis, -1)
    blocks = v.reshape(v.shape[:-1] + (-1, 32))
    amax = np.abs(blocks).max(-1, keepdims=True)
    byte = np.maximum(np.where(amax > 0, np.frexp(amax)[1] - 1 + 127, 0) - down, 1)
    scale = np.exp2(byte - 127.0)
    codes = (blocks / scale).astype(np.float32).astype(dtype).astype(np.float64)
    return np.moveaxis((codes * scale).reshape(v.shape), -1, axis)


WIDE = False


def mx_kscale(k):
    if not WIDE:
        return np.ones(k)
    levels = np.array([10, -10, 5, -5, 0])
    if k % 512:
        return np.exp2(np.random.permutation(np.resize(levels, k // 32))).repeat(32)
    a = np.empty((k // 512, 16))
    for p in range(k // 512):
        a[p, :8] = np.random.permutation(np.resize(levels, 8))
        for g in range(8):
            far = levels[np.abs(levels - a[p, g]) >= 10]
            a[p, g + 8] = far[np.random.randint(len(far))]
    return np.exp2(a.ravel()).repeat(32)


BF16 = ml_dtypes.bfloat16


def bf(x):
    return np.asarray(x, np.float32).astype(BF16)


def f64(x):
    return np.asarray(x).astype(np.float64)


B, N, E, H, NOPE, VDIM, ROPE, QR, KVR = 4, 1024, 1024, 4, 64, 64, 128, 512, 512
KVH = NOPE + VDIM
BASE = 10000.0


def rope(v):
    d = v.shape[-1]
    n = v.shape[-2]
    theta = BASE ** (-2.0 * np.arange(d // 2) / d)
    ang = np.arange(n)[:, None] * theta[None, :]
    cos, sin = np.cos(ang), np.sin(ang)
    v1, v2 = v[..., 0::2], v[..., 1::2]
    return np.stack([v1 * cos - v2 * sin, v1 * sin + v2 * cos], axis=-1).reshape(v.shape)


def setup_inputs():
    s, t = mx_kscale(E), mx_kscale(KVR)
    tcol = np.concatenate([t, np.ones(ROPE)])
    return {"x": bf(np.random.standard_normal((B, N, E)) * s),
            "Wkva": bf(np.random.standard_normal((E, KVR + ROPE)) / np.sqrt(E) / s[:, None] * tcol),
            "Wkvb": bf(np.random.standard_normal((KVR, H * KVH)) / np.sqrt(KVR) / t[:, None])}


def reference(x, Wkva, Wkvb):
    ckv = mxq(f64(x), 2, "e4m3") @ mxq(f64(Wkva), 0, "e4m3")
    compressed, k_pe = ckv[..., :KVR], ckv[..., KVR:]
    k_pe = np.broadcast_to(k_pe[:, None], (B, H, N, ROPE))
    kv = mxq(compressed, 2, "e4m3") @ mxq(f64(Wkvb), 0, "e4m3")
    kv = kv.reshape(B, N, H, KVH).transpose(0, 2, 1, 3)
    k_nope, v = kv[..., :NOPE], kv[..., NOPE:]
    kf = np.concatenate([k_nope, rope(k_pe)], axis=-1)
    return kf, v

@@ -1,0 +1,350 @@
+import math
+from contextlib import ExitStack
+
+import concourse.mybir as mybir
+from concourse.masks import make_identity
+
+F32 = mybir.dt.float32
+BF16 = mybir.dt.bfloat16
+U32 = mybir.dt.uint32
+U8 = mybir.dt.uint8
+I32 = mybir.dt.int32
+FP8X4 = mybir.dt.float8_e4m3fn_x4
+ALU = mybir.AluOpType
+ACT = mybir.ActivationFunctionType
+
+P = 128
+B, N, E, H, NOPE, VDIM, ROPE, KVR = 4, 1024, 1024, 4, 64, 64, 128, 512
+BASE = 10000.0
+WA = KVR + ROPE
+UNITS = 8
+FLOPS = 2 * B * N * E * WA + 2 * B * N * KVR * H * (NOPE + VDIM)
+
+
+def tile_multilatentattention_pb_t_kernel(tc, x, Wkva, Wkvb, out_0, out_1):
+    nc = tc.nc
+    with ExitStack() as ctx:
+        ctx.enter_context(tc.manual_schedule())
+        const = ctx.enter_context(tc.tile_pool(name="const", bufs=1))
+        work = ctx.enter_context(tc.tile_pool(name="work", bufs=2))
+        outp = ctx.enter_context(tc.tile_pool(name="outp", bufs=3))
+        ps_xt = ctx.enter_context(tc.psum_pool(name="ps_xt", bufs=2))
+        ps_mx = ctx.enter_context(tc.psum_pool(name="ps_mx", bufs=4))
+        ps_kv = ctx.enter_context(tc.psum_pool(name="ps_kv", bufs=2))
+
+        wa_raw = const.tile([P, 2, 4, WA], BF16)
+        wb_raw = const.tile([P, 4, 512], BF16)
+        x_sb = []
+        for i in range(UNITS):
+            x_sb.append(const.tile([P, 4, E], BF16, name="x_sb%d" % i))
+        ident = const.tile([P, P], F32)
+        n_i = const.tile([P, 8], I32)
+        n_f = const.tile([P, 8], F32)
+        one = const.tile([P, 1], F32)
+        junk = const.tile([P, 1], F32)
+        u_t = const.tile([P, 64], F32)
+        t_a = const.tile([P, 8, 64], F32)
+        t_b = const.tile([P, 8, 64], F32)
+        t_k = const.tile([P, 8, 64], I32)
+        cs = const.tile([P, 8, 4, 64], F32)
+        wa_g = const.tile([P, 2, WA, 4], BF16, align_bytes=64)
+        wa_c = const.tile([P, 2, WA], U32, align_bytes=64)
+        wa_s = const.tile([P, 2, WA], U8, align_bytes=64)
+        wb_g = const.tile([P, 512, 4], BF16, align_bytes=64)
+        wb_c = const.tile([P, 512], U32, align_bytes=64)
+        wb_s = const.tile([P, 512], U8, align_bytes=64)
+        st = {}
+
+        def copy(eng, out, in_):
+            if eng == "S":
+                nc.scalar.copy(out=out, in_=in_)
+            else:
+                nc.vector.tensor_copy(out=out, in_=in_)
+
+        def load_wa(g):
+            nc.sync.dma_start(
+                out=wa_raw[:, g, :, :],
+                in_=Wkva[512 * g : 512 * (g + 1), :].rearrange("(q t) c -> q t c", t=4),
+            )
+
+        def load_x(i, lo, n):
+            src = x[i // 2].rearrange("(p t) k -> p t k", t=8)
+            t0 = 4 * (i % 2) + lo
+            nc.sync.dma_start(out=x_sb[i][:, lo : lo + n, :], in_=src[:, t0 : t0 + n, :])
+
+        def tables():
+            nc.vector.tensor_scalar_mul(out=u_t[:, 0:1], in0=one[:], scalar1=1.0 / (2.0 * math.pi))
+            s = 1
+            while s < 64:
+                nc.vector.tensor_scalar_mul(out=u_t[:, s : 2 * s], in0=u_t[:, 0:s], scalar1=BASE ** (-2.0 * s / ROPE))
+                s *= 2
+            nc.vector.tensor_copy(out=n_f[:], in_=n_i[:])
+            nc.vector.tensor_tensor(
+                out=t_a[:],
+                in0=n_f[:].unsqueeze(2).to_broadcast([P, 8, 64]),
+                in1=u_t[:].unsqueeze(1).to_broadcast([P, 8, 64]),
+                op=ALU.mult,
+            )
+            nc.vector.tensor_copy(out=t_k[:], in_=t_a[:])
+            nc.vector.tensor_tensor(out=t_a[:], in0=t_a[:], in1=t_k[:], op=ALU.subtract)
+            nc.vector.scalar_tensor_tensor(out=t_b[:], in0=t_a[:], scalar=0.5, in1=t_a[:], op0=ALU.is_gt, op1=ALU.subtract)
+            nc.vector.scalar_tensor_tensor(out=t_a[:], in0=t_b[:], scalar=-1.0, in1=t_b[:], op0=ALU.mult, op1=ALU.min)
+            nc.vector.tensor_scalar_add(out=t_a[:], in0=t_a[:], scalar1=0.25)
+
+        def regroup_a(g, eng, lo, hi):
+            copy(
+                eng,
+                wa_g[:, g, 0:KVR, :].rearrange("p (m q) t -> p q t m", m=4)[:, lo:hi],
+                wa_raw[:, g, :, 0:KVR].rearrange("p t (q m) -> p q t m", m=4)[:, lo:hi],
+            )
+
+        def regroup_r(g, eng):
+            copy(
+                eng,
+                wa_g[:, g, KVR:WA, :].rearrange("p (h i) t -> p h i t", h=2),
+                wa_raw[:, g, :, KVR:WA].rearrange("p t (i h) -> p h i t", h=2),
+            )
+
+        def quant_w(g, lo, hi):
+            nc.vector.quantize_mx(
+                out=wa_c[:, g, lo:hi].bitcast(FP8X4),
+                scales=wa_s[:, g, lo:hi],
+                in_=wa_g[:, g, lo:hi, :].rearrange("p w t -> p (w t)"),
+            )
+
+        def regroup_b(eng, s):
+            copy(
+                eng,
+                wb_g[:, 256 * s : 256 * (s + 1), :].rearrange("p (h c) t -> p h c t", h=H),
+                wb_raw[:].rearrange("p t (h s c) -> p s h c t", h=H, s=2)[:, s],
+            )
+
+        def transposes(i, q):
+            pr, g = q // 2, q % 2
+            xt = ps_xt.tile([P, 2, 256], F32, name="xt")
+            for u in range(2):
+                for jj in range(2):
+                    nc.tensor.transpose(
+                        xt[:, u, 128 * jj : 128 * (jj + 1)],
+                        x_sb[i][:, 2 * pr + jj, :].bitcast(F32)[:, 256 * g + u : 256 * (g + 1) : 2],
+                        ident[:],
+                    )
+            st[("xt", i, q)] = xt
+            if q == 0:
+                st[("xg", i)] = work.tile([P, 2048], F32, name="xg", align_bytes=64)
+                st[("xc", i)] = work.tile([P, 1024], U32, name="xc", align_bytes=64)
+                st[("xs", i)] = work.tile([P, 1024], U8, name="xs", align_bytes=64)
+
+        def x_out(i, q, eng):
+            copy(
+                eng,
+                st[("xg", i)][:, 512 * q : 512 * (q + 1)].rearrange("p (r u) -> p r u", u=2),
+                st[("xt", i, q)][:].rearrange("p u r -> p r u"),
+            )
+
+        def quant_x(i, pr):
+            nc.vector.quantize_mx(
+                out=st[("xc", i)][:, 512 * pr : 512 * (pr + 1)].bitcast(FP8X4),
+                scales=st[("xs", i)][:, 512 * pr : 512 * (pr + 1)],
+                in_=st[("xg", i)][:, 1024 * pr : 1024 * (pr + 1)].bitcast(BF16),
+            )
+
+        def x_cols(j, g):
+            c0 = ((j // 2) * 2 + g) * 256 + (j % 2) * 128
+            return slice(c0, c0 + 128)
+
+        def rope_mm(i):
+            kp = ps_mx.tile([P, 4, 128], F32, name="mx")
+            for j in range(4):
+                for g in range(2):
+                    nc.tensor.matmul_mx(
+                        out=kp[:, j, :],
+                        lhsT=st[("xc", i)][:, x_cols(j, g)].bitcast(FP8X4),
+                        lhsT_scale=st[("xs", i)][:, x_cols(j, g)],
+                        rhs=wa_c[:, g, KVR:WA].bitcast(FP8X4),
+                        rhs_scale=wa_s[:, g, KVR:WA],
+                        start=(g == 0),
+                        stop=(g == 1),
+                    )
+            st[("kp", i)] = kp
+            st[("kf", i)] = outp.tile([P, H, 4, NOPE + ROPE], F32, name="kf")
+            st[("vv", i)] = outp.tile([P, H, 4, VDIM], F32, name="vv")
+
+        def rope_mul(i):
+            pt = work.tile([P, 4, 2, 2, 64], F32, name="pt")
+            t0 = 4 * (i % 2)
+            nc.vector.tensor_tensor(
+                out=pt[:].rearrange("p t h r c -> p (t h) r c"),
+                in0=st[("kp", i)][:].rearrange("p t (h c) -> p (t h) c", h=2).unsqueeze(2).to_broadcast([P, 8, 2, 64]),
+                in1=cs[:, t0 : t0 + 4, :, :].rearrange("p t (h r) c -> p (t h) r c", h=2),
+                op=ALU.mult,
+            )
+            st[("pt", i)] = pt
+
+        def rope_add(i):
+            pt = st[("pt", i)]
+            nc.vector.tensor_tensor(
+                out=st[("kf", i)][:, 0, :, NOPE:].rearrange("p t (c r) -> p t c r", r=2),
+                in0=pt[:, :, 0, :, :].rearrange("p t r c -> p t c r"),
+                in1=pt[:, :, 1, :, :].rearrange("p t r c -> p t c r"),
+                op=ALU.add,
+            )
+
+        def rope_rep(i):
+            kf = st[("kf", i)]
+            nc.vector.tensor_copy(
+                out=kf[:, 1:H, :, NOPE:].rearrange("p h t c -> p t h c"),
+                in_=kf[:, 0, :, NOPE:].unsqueeze(2).to_broadcast([P, 4, H - 1, ROPE]),
+            )
+
+        def latent_mm(i, j):
+            ct = ps_mx.tile([P, 4, 128], F32, name="mx")
+            for m in range(4):
+                for g in range(2):
+                    nc.tensor.matmul_mx(
+                        out=ct[:, m, :],
+                        lhsT=wa_c[:, g, 128 * m : 128 * (m + 1)].bitcast(FP8X4),
+                        lhsT_scale=wa_s[:, g, 128 * m : 128 * (m + 1)],
+                        rhs=st[("xc", i)][:, x_cols(j, g)].bitcast(FP8X4),
+                        rhs_scale=st[("xs", i)][:, x_cols(j, g)],
+                        start=(g == 0),
+                        stop=(g == 1),
+                    )
+            st[("ct", i, j)] = ct
+            if j == 0:
+                st[("cg", i)] = work.tile([P, 512, 4], BF16, name="cg", align_bytes=64)
+
+        def c_out(i, j, eng):
+            copy(eng, st[("cg", i)][:, 128 * j : 128 * (j + 1), :], st[("ct", i, j)][:].rearrange("p m r -> p r m"))
+
+        def quant_c(i, pr):
+            if pr == 0:
+                st[("cc", i)] = work.tile([P, 512], U32, name="cc", align_bytes=64)
+                st[("cs", i)] = work.tile([P, 512], U8, name="csc", align_bytes=64)
+            nc.vector.quantize_mx(
+                out=st[("cc", i)][:, 256 * pr : 256 * (pr + 1)].bitcast(FP8X4),
+                scales=st[("cs", i)][:, 256 * pr : 256 * (pr + 1)],
+                in_=st[("cg", i)][:, 256 * pr : 256 * (pr + 1), :].rearrange("p w t -> p (w t)"),
+            )
+
+        def kv_mm_out(i, pr, eng_k, eng_v):
+            banks = []
+            for s in range(2):
+                banks.append(ps_kv.tile([P, 2, H, 64], F32, name="kv"))
+            for jj in range(2):
+                j = 2 * pr + jj
+                for s in range(2):
+                    nc.tensor.matmul_mx(
+                        out=banks[s][:, jj, :, :].rearrange("p h c -> p (h c)"),
+                        lhsT=st[("cc", i)][:, 128 * j : 128 * (j + 1)].bitcast(FP8X4),
+                        lhsT_scale=st[("cs", i)][:, 128 * j : 128 * (j + 1)],
+                        rhs=wb_c[:, 256 * s : 256 * (s + 1)].bitcast(FP8X4),
+                        rhs_scale=wb_s[:, 256 * s : 256 * (s + 1)],
+                        start=True,
+                        stop=True,
+                    )
+            copy(eng_k, st[("kf", i)][:, :, 2 * pr : 2 * pr + 2, 0:NOPE].rearrange("p h j c -> p j h c"), banks[0][:])
+            copy(eng_v, st[("vv", i)][:, :, 2 * pr : 2 * pr + 2, :].rearrange("p h j c -> p j h c"), banks[1][:])
+
+        def store(i, j_lo, j_n):
+            b = i // 2
+            t0 = 4 * (i % 2) + j_lo
+            nc.sync.dma_start(
+                out=out_0[b].rearrange("h (p t) f -> p h t f", t=8)[:, :, t0 : t0 + j_n, :],
+                in_=st[("kf", i)][:, :, j_lo : j_lo + j_n, :],
+            )
+            nc.sync.dma_start(
+                out=out_1[b].rearrange("h (p t) f -> p h t f", t=8)[:, :, t0 : t0 + j_n, :],
+                in_=st[("vv", i)][:, :, j_lo : j_lo + j_n, :],
+            )
+
+        load_wa(0)
+        load_x(0, 0, 2)
+        load_wa(1)
+        load_x(0, 2, 2)
+        nc.sync.dma_start(out=wb_raw[:], in_=Wkvb.rearrange("(p t) n -> p t n", t=4))
+        for i in range(1, UNITS):
+            load_x(i, 0, 4)
+        nc.gpsimd.iota(out=n_i[:], pattern=[[1, 8]], base=0, channel_multiplier=8)
+        make_identity(nc, ident[:])
+        nc.vector.memset(one[:], 1.0)
+        nc.scalar.activation(out=junk[:], in_=one[:], func=ACT.Sin)
+        tables()
+        nc.scalar.activation(out=cs[:, :, 0, :], in_=t_a[:], func=ACT.Sin, scale=2.0 * math.pi)
+        nc.scalar.activation(out=cs[:, :, 1, :], in_=t_b[:], func=ACT.Sin, scale=-2.0 * math.pi)
+        regroup_a(0, "V", 0, 128)
+        transposes(0, 0)
+        transposes(0, 1)
+        x_out(0, 0, "S")
+        x_out(0, 1, "S")
+        quant_w(0, 0, KVR)
+        regroup_a(1, "V", 0, 88)
+        regroup_a(1, "S", 88, 128)
+        quant_x(0, 0)
+        quant_w(1, 0, KVR)
+        transposes(0, 2)
+        transposes(0, 3)
+        regroup_r(0, "S")
+        x_out(0, 2, "S")
+        x_out(0, 3, "S")
+        regroup_r(1, "S")
+        quant_x(0, 1)
+        quant_w(0, KVR, WA)
+        quant_w(1, KVR, WA)
+        nc.vector.tensor_scalar_mul(out=cs[:, :, 2, :], in0=cs[:, :, 1, :], scalar1=-1.0)
+        nc.vector.tensor_copy(out=cs[:, :, 3, :], in_=cs[:, :, 0, :])
+
+        for i in range(UNITS + 1):
+            nxt = i + 1 < UNITS
+            cur = i < UNITS
+            prv = i >= 1
+            last = i == UNITS
+            if prv:
+                quant_c(i - 1, 1)
+            if cur:
+                latent_mm(i, 0)
+                c_out(i, 0, "V")
+                latent_mm(i, 1)
+                c_out(i, 1, "S")
+            if nxt:
+                transposes(i + 1, 0)
+                transposes(i + 1, 1)
+                x_out(i + 1, 0, "S")
+                x_out(i + 1, 1, "S")
+            if prv:
+                if not last:
+                    rope_rep(i - 1)
+                kv_mm_out(i - 1, 1, "S", "V" if last else "S")
+                if last:
+                    store(i - 1, 2, 2)
+                else:
+                    store(i - 1, 0, 4)
+            if cur:
+                quant_c(i, 0)
+            if i == 0:
+                regroup_b("V", 0)
+                regroup_b("S", 1)
+                nc.vector.quantize_mx(out=wb_c[:].bitcast(FP8X4), scales=wb_s[:], in_=wb_g[:].rearrange("p w t -> p (w t)"))
+            if nxt:
+                quant_x(i + 1, 0)
+            if cur:
+                rope_mm(i)
+                rope_mul(i)
+                latent_mm(i, 2)
+                c_out(i, 2, "V")
+                rope_add(i)
+            if nxt:
+                transposes(i + 1, 2)
+                transposes(i + 1, 3)
+                x_out(i + 1, 2, "S")
+                x_out(i + 1, 3, "S")
+            if cur:
+                latent_mm(i, 3)
+                c_out(i, 3, "S")
+                if i == UNITS - 1:
+                    rope_rep(i)
+                kv_mm_out(i, 0, "S", "S")
+                if i == UNITS - 1:
+                    store(i, 0, 2)
+            if nxt:
+                quant_x(i + 1, 1)

@@ -38,10 +38,10 @@ def tile_multilatentattention_pb_t_kernel(tc, x, Wkva, Wkvb, out_0, out_1):
         for i in range(UNITS):
             x_sb.append(const.tile([P, 4, E], BF16, name="x_sb%d" % i))
         ident = const.tile([P, P], F32)
-        n_i = const.tile([P, 8], I32)
         n_f = const.tile([P, 8], F32)
         one = const.tile([P, 1], F32)
         junk = const.tile([P, 1], F32)
+        half_pi = const.tile([P, 1], F32)
         u_t = const.tile([P, 64], F32)
         t_a = const.tile([P, 8, 64], F32)
         t_b = const.tile([P, 8, 64], F32)
@@ -78,7 +78,6 @@ def tile_multilatentattention_pb_t_kernel(tc, x, Wkva, Wkvb, out_0, out_1):
             while s < 64:
                 nc.vector.tensor_scalar_mul(out=u_t[:, s : 2 * s], in0=u_t[:, 0:s], scalar1=BASE ** (-2.0 * s / ROPE))
                 s *= 2
-            nc.vector.tensor_copy(out=n_f[:], in_=n_i[:])
             nc.vector.tensor_tensor(
                 out=t_a[:],
                 in0=n_f[:].unsqueeze(2).to_broadcast([P, 8, 64]),
@@ -87,9 +86,12 @@ def tile_multilatentattention_pb_t_kernel(tc, x, Wkva, Wkvb, out_0, out_1):
             )
             nc.vector.tensor_copy(out=t_k[:], in_=t_a[:])
             nc.vector.tensor_tensor(out=t_a[:], in0=t_a[:], in1=t_k[:], op=ALU.subtract)
-            nc.vector.scalar_tensor_tensor(out=t_b[:], in0=t_a[:], scalar=0.5, in1=t_a[:], op0=ALU.is_gt, op1=ALU.subtract)
-            nc.vector.scalar_tensor_tensor(out=t_a[:], in0=t_b[:], scalar=-1.0, in1=t_b[:], op0=ALU.mult, op1=ALU.min)
-            nc.vector.tensor_scalar_add(out=t_a[:], in0=t_a[:], scalar1=0.25)
+
+        def cosines(k):
+            nc.scalar.activation(out=cs[:, :, k, :], in_=t_b[:], func=ACT.Sin, scale=-2.0 * math.pi, bias=half_pi[:])
+
+        def sines(k, sign):
+            nc.scalar.activation(out=cs[:, :, k, :], in_=t_a[:], func=ACT.Sin, scale=sign * 2.0 * math.pi)
 
         def regroup_a(g, eng, lo, hi):
             copy(
@@ -265,34 +267,36 @@ def tile_multilatentattention_pb_t_kernel(tc, x, Wkva, Wkvb, out_0, out_1):
         nc.sync.dma_start(out=wb_raw[:], in_=Wkvb.rearrange("(p t) n -> p t n", t=4))
         for i in range(1, UNITS):
             load_x(i, 0, 4)
-        nc.gpsimd.iota(out=n_i[:], pattern=[[1, 8]], base=0, channel_multiplier=8)
-        make_identity(nc, ident[:])
         nc.vector.memset(one[:], 1.0)
+        nc.gpsimd.iota(out=n_f[:], pattern=[[1, 8]], base=0, channel_multiplier=8, allow_small_or_imprecise_dtypes=True)
+        make_identity(nc, ident[:])
         nc.scalar.activation(out=junk[:], in_=one[:], func=ACT.Sin)
+        nc.scalar.mul(out=half_pi[:], in_=one[:], mul=math.pi / 2.0)
         tables()
-        nc.scalar.activation(out=cs[:, :, 0, :], in_=t_a[:], func=ACT.Sin, scale=2.0 * math.pi)
-        nc.scalar.activation(out=cs[:, :, 1, :], in_=t_b[:], func=ACT.Sin, scale=-2.0 * math.pi)
+        nc.scalar.activation(out=t_b[:], in_=t_a[:], func=ACT.Abs)
+        cosines(0)
+        sines(1, 1.0)
+        sines(2, -1.0)
         regroup_a(0, "V", 0, 128)
         transposes(0, 0)
         transposes(0, 1)
         x_out(0, 0, "S")
         x_out(0, 1, "S")
         quant_w(0, 0, KVR)
-        regroup_a(1, "V", 0, 88)
-        regroup_a(1, "S", 88, 128)
+        regroup_a(1, "V", 0, 96)
+        regroup_a(1, "S", 96, 128)
         quant_x(0, 0)
         quant_w(1, 0, KVR)
         transposes(0, 2)
         transposes(0, 3)
-        regroup_r(0, "S")
         x_out(0, 2, "S")
         x_out(0, 3, "S")
+        regroup_r(0, "S")
         regroup_r(1, "S")
+        cosines(3)
         quant_x(0, 1)
         quant_w(0, KVR, WA)
         quant_w(1, KVR, WA)
-        nc.vector.tensor_scalar_mul(out=cs[:, :, 2, :], in0=cs[:, :, 1, :], scalar1=-1.0)
-        nc.vector.tensor_copy(out=cs[:, :, 3, :], in_=cs[:, :, 0, :])
 
         for i in range(UNITS + 1):
             nxt = i + 1 < UNITS
@@ -312,10 +316,10 @@ def tile_multilatentattention_pb_t_kernel(tc, x, Wkva, Wkvb, out_0, out_1):
                 x_out(i + 1, 0, "S")
                 x_out(i + 1, 1, "S")
             if prv:
-                if not last:
+                if i <= UNITS - 3:
                     rope_rep(i - 1)
                 kv_mm_out(i - 1, 1, "S", "V" if last else "S")
-                if last:
+                if i > UNITS - 3:
                     store(i - 1, 2, 2)
                 else:
                     store(i - 1, 0, 4)
@@ -341,10 +345,10 @@ def tile_multilatentattention_pb_t_kernel(tc, x, Wkva, Wkvb, out_0, out_1):
             if cur:
                 latent_mm(i, 3)
                 c_out(i, 3, "S")
-                if i == UNITS - 1:
+                if i >= UNITS - 3:
                     rope_rep(i)
                 kv_mm_out(i, 0, "S", "S")
-                if i == UNITS - 1:
+                if i >= UNITS - 3:
                     store(i, 0, 2)
             if nxt:
                 quant_x(i + 1, 1)

@@ -18,6 +18,7 @@ B, N, E, H, NOPE, VDIM, ROPE, KVR = 4, 1024, 1024, 4, 64, 64, 128, 512
 BASE = 10000.0
 WA = KVR + ROPE
 UNITS = 8
+FIRST_PERM = 2
 FLOPS = 2 * B * N * E * WA + 2 * B * N * KVR * H * (NOPE + VDIM)
 
 
@@ -28,6 +29,7 @@ def tile_multilatentattention_pb_t_kernel(tc, x, Wkva, Wkvb, out_0, out_1):
         const = ctx.enter_context(tc.tile_pool(name="const", bufs=1))
         work = ctx.enter_context(tc.tile_pool(name="work", bufs=2))
         outp = ctx.enter_context(tc.tile_pool(name="outp", bufs=3))
+        xpp = ctx.enter_context(tc.tile_pool(name="xpp", bufs=2))
         ps_xt = ctx.enter_context(tc.psum_pool(name="ps_xt", bufs=2))
         ps_mx = ctx.enter_context(tc.psum_pool(name="ps_mx", bufs=4))
         ps_kv = ctx.enter_context(tc.psum_pool(name="ps_kv", bufs=2))
@@ -121,6 +123,12 @@ def tile_multilatentattention_pb_t_kernel(tc, x, Wkva, Wkvb, out_0, out_1):
                 wb_raw[:].rearrange("p t (h s c) -> p s h c t", h=H, s=2)[:, s],
             )
 
+        def cols(i, t, g, u):
+            if ("xp", i) in st:
+                c0 = 256 * g + 128 * u
+                return st[("xp", i)][:, t, c0 : c0 + 128]
+            return x_sb[i][:, t, :].bitcast(F32)[:, 256 * g + u : 256 * (g + 1) : 2]
+
         def transposes(i, q):
             pr, g = q // 2, q % 2
             xt = ps_xt.tile([P, 2, 256], F32, name="xt")
@@ -128,7 +136,7 @@ def tile_multilatentattention_pb_t_kernel(tc, x, Wkva, Wkvb, out_0, out_1):
                 for jj in range(2):
                     nc.tensor.transpose(
                         xt[:, u, 128 * jj : 128 * (jj + 1)],
-                        x_sb[i][:, 2 * pr + jj, :].bitcast(F32)[:, 256 * g + u : 256 * (g + 1) : 2],
+                        cols(i, 2 * pr + jj, g, u),
                         ident[:],
                     )
             st[("xt", i, q)] = xt
@@ -229,15 +237,14 @@ def tile_multilatentattention_pb_t_kernel(tc, x, Wkva, Wkvb, out_0, out_1):
                 in_=st[("cg", i)][:, 256 * pr : 256 * (pr + 1), :].rearrange("p w t -> p (w t)"),
             )
 
-        def kv_mm_out(i, pr, eng_k, eng_v):
-            banks = []
+        def kv_mm(i, pr):
             for s in range(2):
-                banks.append(ps_kv.tile([P, 2, H, 64], F32, name="kv"))
-            for jj in range(2):
-                j = 2 * pr + jj
-                for s in range(2):
+                bank = ps_kv.tile([P, 2, H, 64], F32, name="kv")
+                st[("kv", i, pr, s)] = bank
+                for jj in range(2):
+                    j = 2 * pr + jj
                     nc.tensor.matmul_mx(
-                        out=banks[s][:, jj, :, :].rearrange("p h c -> p (h c)"),
+                        out=bank[:, jj, :, :].rearrange("p h c -> p (h c)"),
                         lhsT=st[("cc", i)][:, 128 * j : 128 * (j + 1)].bitcast(FP8X4),
                         lhsT_scale=st[("cs", i)][:, 128 * j : 128 * (j + 1)],
                         rhs=wb_c[:, 256 * s : 256 * (s + 1)].bitcast(FP8X4),
@@ -245,35 +252,61 @@ def tile_multilatentattention_pb_t_kernel(tc, x, Wkva, Wkvb, out_0, out_1):
                         start=True,
                         stop=True,
                     )
-            copy(eng_k, st[("kf", i)][:, :, 2 * pr : 2 * pr + 2, 0:NOPE].rearrange("p h j c -> p j h c"), banks[0][:])
-            copy(eng_v, st[("vv", i)][:, :, 2 * pr : 2 * pr + 2, :].rearrange("p h j c -> p j h c"), banks[1][:])
 
-        def store(i, j_lo, j_n):
+        def kv_out(i, pr, s, eng):
+            dst = st[("kf", i)][:, :, 2 * pr : 2 * pr + 2, 0:NOPE] if s == 0 else st[("vv", i)][:, :, 2 * pr : 2 * pr + 2, :]
+            copy(eng, dst.rearrange("p h j c -> p j h c"), st[("kv", i, pr, s)][:])
+
+        def store_kf(i, lo, n):
             b = i // 2
-            t0 = 4 * (i % 2) + j_lo
+            t0 = 4 * (i % 2) + lo
             nc.sync.dma_start(
-                out=out_0[b].rearrange("h (p t) f -> p h t f", t=8)[:, :, t0 : t0 + j_n, :],
-                in_=st[("kf", i)][:, :, j_lo : j_lo + j_n, :],
+                out=out_0[b].rearrange("h (p t) f -> p h t f", t=8)[:, :, t0 : t0 + n, :],
+                in_=st[("kf", i)][:, :, lo : lo + n, :],
             )
+
+        def store_vv(i, lo, n):
+            b = i // 2
+            t0 = 4 * (i % 2) + lo
             nc.sync.dma_start(
-                out=out_1[b].rearrange("h (p t) f -> p h t f", t=8)[:, :, t0 : t0 + j_n, :],
-                in_=st[("vv", i)][:, :, j_lo : j_lo + j_n, :],
+                out=out_1[b].rearrange("h (p t) f -> p h t f", t=8)[:, :, t0 : t0 + n, :],
+                in_=st[("vv", i)][:, :, lo : lo + n, :],
+            )
+
+        def quant_b():
+            nc.vector.quantize_mx(out=wb_c[:].bitcast(FP8X4), scales=wb_s[:], in_=wb_g[:].rearrange("p w t -> p (w t)"))
+
+        def load_b():
+            nc.sync.dma_start(out=wb_raw[:], in_=Wkvb.rearrange("(p t) n -> p t n", t=4))
+
+        def consts():
+            nc.vector.memset(one[:], 1.0)
+            nc.gpsimd.iota(out=n_f[:], pattern=[[1, 8]], base=0, channel_multiplier=8, allow_small_or_imprecise_dtypes=True)
+            make_identity(nc, ident[:])
+            nc.scalar.activation(out=junk[:], in_=one[:], func=ACT.Sin)
+            nc.scalar.mul(out=half_pi[:], in_=one[:], mul=math.pi / 2.0)
+
+        def absf():
+            nc.scalar.activation(out=t_b[:], in_=t_a[:], func=ACT.Abs)
+
+        def permute(i, pr):
+            if pr == 0:
+                st[("xp", i)] = xpp.tile([P, 4, 512], F32, name="xp")
+            nc.vector.tensor_copy(
+                out=st[("xp", i)][:, 2 * pr : 2 * pr + 2, :].rearrange("p t (g u w) -> p (t g) u w", g=2, u=2),
+                in_=x_sb[i][:, 2 * pr : 2 * pr + 2, :].bitcast(F32).rearrange("p t (g w u) -> p (t g) u w", g=2, u=2),
             )
 
         load_wa(0)
         load_x(0, 0, 2)
         load_wa(1)
         load_x(0, 2, 2)
-        nc.sync.dma_start(out=wb_raw[:], in_=Wkvb.rearrange("(p t) n -> p t n", t=4))
+        load_b()
         for i in range(1, UNITS):
             load_x(i, 0, 4)
-        nc.vector.memset(one[:], 1.0)
-        nc.gpsimd.iota(out=n_f[:], pattern=[[1, 8]], base=0, channel_multiplier=8, allow_small_or_imprecise_dtypes=True)
-        make_identity(nc, ident[:])
-        nc.scalar.activation(out=junk[:], in_=one[:], func=ACT.Sin)
-        nc.scalar.mul(out=half_pi[:], in_=one[:], mul=math.pi / 2.0)
+        consts()
         tables()
-        nc.scalar.activation(out=t_b[:], in_=t_a[:], func=ACT.Abs)
+        absf()
         cosines(0)
         sines(1, 1.0)
         sines(2, -1.0)
@@ -298,57 +331,55 @@ def tile_multilatentattention_pb_t_kernel(tc, x, Wkva, Wkvb, out_0, out_1):
         quant_w(0, KVR, WA)
         quant_w(1, KVR, WA)
 
-        for i in range(UNITS + 1):
-            nxt = i + 1 < UNITS
-            cur = i < UNITS
-            prv = i >= 1
-            last = i == UNITS
-            if prv:
-                quant_c(i - 1, 1)
-            if cur:
-                latent_mm(i, 0)
-                c_out(i, 0, "V")
-                latent_mm(i, 1)
-                c_out(i, 1, "S")
-            if nxt:
-                transposes(i + 1, 0)
-                transposes(i + 1, 1)
-                x_out(i + 1, 0, "S")
-                x_out(i + 1, 1, "S")
-            if prv:
-                if i <= UNITS - 3:
-                    rope_rep(i - 1)
-                kv_mm_out(i - 1, 1, "S", "V" if last else "S")
-                if i > UNITS - 3:
-                    store(i - 1, 2, 2)
-                else:
-                    store(i - 1, 0, 4)
-            if cur:
-                quant_c(i, 0)
-            if i == 0:
+        for n in range(UNITS + 1):
+            if n >= 1:
+                quant_c(n - 1, 1)
+            if n < UNITS:
+                latent_mm(n, 0)
+                c_out(n, 0, "S")
+                latent_mm(n, 1)
+            if n >= 1:
+                rope_add(n - 1)
+            if n < UNITS:
+                c_out(n, 1, "V")
+            if n + 1 < UNITS:
+                transposes(n + 1, 0)
+                transposes(n + 1, 1)
+                x_out(n + 1, 0, "S")
+                x_out(n + 1, 1, "S")
+            if n >= 1:
+                rope_rep(n - 1)
+                kv_mm(n - 1, 1)
+                kv_out(n - 1, 1, 1, "S")
+                store_vv(n - 1, 0, 4)
+                kv_out(n - 1, 1, 0, "S")
+                store_kf(n - 1, 0, 4)
+            if n < UNITS:
+                quant_c(n, 0)
+            if n == 0:
                 regroup_b("V", 0)
                 regroup_b("S", 1)
-                nc.vector.quantize_mx(out=wb_c[:].bitcast(FP8X4), scales=wb_s[:], in_=wb_g[:].rearrange("p w t -> p (w t)"))
-            if nxt:
-                quant_x(i + 1, 0)
-            if cur:
-                rope_mm(i)
-                rope_mul(i)
-                latent_mm(i, 2)
-                c_out(i, 2, "V")
-                rope_add(i)
-            if nxt:
-                transposes(i + 1, 2)
-                transposes(i + 1, 3)
-                x_out(i + 1, 2, "S")
-                x_out(i + 1, 3, "S")
-            if cur:
-                latent_mm(i, 3)
-                c_out(i, 3, "S")
-                if i >= UNITS - 3:
-                    rope_rep(i)
-                kv_mm_out(i, 0, "S", "S")
-                if i >= UNITS - 3:
-                    store(i, 0, 2)
-            if nxt:
-                quant_x(i + 1, 1)
+                quant_b()
+            if n + 1 < UNITS:
+                quant_x(n + 1, 0)
+            if FIRST_PERM <= n + 2 < UNITS:
+                permute(n + 2, 0)
+                permute(n + 2, 1)
+            if n < UNITS:
+                rope_mm(n)
+                latent_mm(n, 2)
+                c_out(n, 2, "S")
+                rope_mul(n)
+            if n + 1 < UNITS:
+                transposes(n + 1, 2)
+                transposes(n + 1, 3)
+                x_out(n + 1, 2, "S")
+                x_out(n + 1, 3, "S")
+            if n < UNITS:
+                latent_mm(n, 3)
+                c_out(n, 3, "S")
+                kv_mm(n, 0)
+                kv_out(n, 0, 0, "S")
+                kv_out(n, 0, 1, "S")
+            if n + 1 < UNITS:
+                quant_x(n + 1, 1)

@@ -18,7 +18,6 @@ B, N, E, H, NOPE, VDIM, ROPE, KVR = 4, 1024, 1024, 4, 64, 64, 128, 512
 BASE = 10000.0
 WA = KVR + ROPE
 UNITS = 8
-FIRST_PERM = 2
 FLOPS = 2 * B * N * E * WA + 2 * B * N * KVR * H * (NOPE + VDIM)
 
 
@@ -152,11 +151,11 @@ def tile_multilatentattention_pb_t_kernel(tc, x, Wkva, Wkvb, out_0, out_1):
                 st[("xt", i, q)][:].rearrange("p u r -> p r u"),
             )
 
-        def quant_x(i, pr):
+        def quant_x(i, lo, n):
             nc.vector.quantize_mx(
-                out=st[("xc", i)][:, 512 * pr : 512 * (pr + 1)].bitcast(FP8X4),
-                scales=st[("xs", i)][:, 512 * pr : 512 * (pr + 1)],
-                in_=st[("xg", i)][:, 1024 * pr : 1024 * (pr + 1)].bitcast(BF16),
+                out=st[("xc", i)][:, 512 * lo : 512 * (lo + n)].bitcast(FP8X4),
+                scales=st[("xs", i)][:, 512 * lo : 512 * (lo + n)],
+                in_=st[("xg", i)][:, 1024 * lo : 1024 * (lo + n)].bitcast(BF16),
             )
 
         def x_cols(j, g):
@@ -227,14 +226,14 @@ def tile_multilatentattention_pb_t_kernel(tc, x, Wkva, Wkvb, out_0, out_1):
         def c_out(i, j, eng):
             copy(eng, st[("cg", i)][:, 128 * j : 128 * (j + 1), :], st[("ct", i, j)][:].rearrange("p m r -> p r m"))
 
-        def quant_c(i, pr):
-            if pr == 0:
+        def quant_c(i, lo, n):
+            if lo == 0:
                 st[("cc", i)] = work.tile([P, 512], U32, name="cc", align_bytes=64)
                 st[("cs", i)] = work.tile([P, 512], U8, name="csc", align_bytes=64)
             nc.vector.quantize_mx(
-                out=st[("cc", i)][:, 256 * pr : 256 * (pr + 1)].bitcast(FP8X4),
-                scales=st[("cs", i)][:, 256 * pr : 256 * (pr + 1)],
-                in_=st[("cg", i)][:, 256 * pr : 256 * (pr + 1), :].rearrange("p w t -> p (w t)"),
+                out=st[("cc", i)][:, 256 * lo : 256 * (lo + n)].bitcast(FP8X4),
+                scales=st[("cs", i)][:, 256 * lo : 256 * (lo + n)],
+                in_=st[("cg", i)][:, 256 * lo : 256 * (lo + n), :].rearrange("p w t -> p (w t)"),
             )
 
         def kv_mm(i, pr):
@@ -289,27 +288,25 @@ def tile_multilatentattention_pb_t_kernel(tc, x, Wkva, Wkvb, out_0, out_1):
         def absf():
             nc.scalar.activation(out=t_b[:], in_=t_a[:], func=ACT.Abs)
 
-        def permute(i, pr):
-            if pr == 0:
-                st[("xp", i)] = xpp.tile([P, 4, 512], F32, name="xp")
+        def permute(i):
+            st[("xp", i)] = xpp.tile([P, 4, 512], F32, name="xp")
             nc.vector.tensor_copy(
-                out=st[("xp", i)][:, 2 * pr : 2 * pr + 2, :].rearrange("p t (g u w) -> p (t g) u w", g=2, u=2),
-                in_=x_sb[i][:, 2 * pr : 2 * pr + 2, :].bitcast(F32).rearrange("p t (g w u) -> p (t g) u w", g=2, u=2),
+                out=st[("xp", i)][:].rearrange("p t (g u w) -> p (t g) u w", g=2, u=2),
+                in_=x_sb[i][:].bitcast(F32).rearrange("p t (g w u) -> p (t g) u w", g=2, u=2),
             )
 
         load_wa(0)
         load_x(0, 0, 2)
         load_wa(1)
         load_x(0, 2, 2)
+        load_x(1, 0, 4)
         load_b()
-        for i in range(1, UNITS):
+        for i in range(2, UNITS):
             load_x(i, 0, 4)
         consts()
         tables()
         absf()
         cosines(0)
-        sines(1, 1.0)
-        sines(2, -1.0)
         regroup_a(0, "V", 0, 128)
         transposes(0, 0)
         transposes(0, 1)
@@ -318,25 +315,28 @@ def tile_multilatentattention_pb_t_kernel(tc, x, Wkva, Wkvb, out_0, out_1):
         quant_w(0, 0, KVR)
         regroup_a(1, "V", 0, 96)
         regroup_a(1, "S", 96, 128)
-        quant_x(0, 0)
+        quant_x(0, 0, 1)
         quant_w(1, 0, KVR)
         transposes(0, 2)
         transposes(0, 3)
+        sines(1, 1.0)
         x_out(0, 2, "S")
         x_out(0, 3, "S")
-        regroup_r(0, "S")
-        regroup_r(1, "S")
-        cosines(3)
-        quant_x(0, 1)
+        regroup_r(0, "V")
+        regroup_r(1, "V")
+        sines(2, -1.0)
+        quant_x(0, 1, 1)
         quant_w(0, KVR, WA)
         quant_w(1, KVR, WA)
 
         for n in range(UNITS + 1):
             if n >= 1:
-                quant_c(n - 1, 1)
+                quant_c(n - 1, 1, 1)
             if n < UNITS:
                 latent_mm(n, 0)
                 c_out(n, 0, "S")
+                if n == 0:
+                    cosines(3)
                 latent_mm(n, 1)
             if n >= 1:
                 rope_add(n - 1)
@@ -355,26 +355,25 @@ def tile_multilatentattention_pb_t_kernel(tc, x, Wkva, Wkvb, out_0, out_1):
                 kv_out(n - 1, 1, 0, "S")
                 store_kf(n - 1, 0, 4)
             if n < UNITS:
-                quant_c(n, 0)
-            if n == 0:
-                regroup_b("V", 0)
-                regroup_b("S", 1)
-                quant_b()
-            if n + 1 < UNITS:
-                quant_x(n + 1, 0)
-            if FIRST_PERM <= n + 2 < UNITS:
-                permute(n + 2, 0)
-                permute(n + 2, 1)
-            if n < UNITS:
+                quant_c(n, 0, 1)
                 rope_mm(n)
+                rope_mul(n)
+                if n == 0:
+                    regroup_b("V", 0)
+                    regroup_b("V", 1)
+                    quant_b()
+            if n + 1 < UNITS:
+                quant_x(n + 1, 0, 1)
+            if (n + 2) % 2 == 1 and 3 <= n + 2 < UNITS:
+                permute(n + 2)
+            if n < UNITS:
                 latent_mm(n, 2)
                 c_out(n, 2, "S")
-                rope_mul(n)
             if n + 1 < UNITS:
                 transposes(n + 1, 2)
                 transposes(n + 1, 3)
                 x_out(n + 1, 2, "S")
-                x_out(n + 1, 3, "S")
+                x_out(n + 1, 3, "V" if n % 2 == 0 else "S")
             if n < UNITS:
                 latent_mm(n, 3)
                 c_out(n, 3, "S")
@@ -382,4 +381,4 @@ def tile_multilatentattention_pb_t_kernel(tc, x, Wkva, Wkvb, out_0, out_1):
                 kv_out(n, 0, 0, "S")
                 kv_out(n, 0, 1, "S")
             if n + 1 < UNITS:
-                quant_x(n + 1, 1)
+                quant_x(n + 1, 1, 1)

@@ -18,6 +18,8 @@ B, N, E, H, NOPE, VDIM, ROPE, KVR = 4, 1024, 1024, 4, 64, 64, 128, 512
 BASE = 10000.0
 WA = KVR + ROPE
 UNITS = 8
+FIRST_HALF = 5
+FIRST_HALF_V = 8
 FLOPS = 2 * B * N * E * WA + 2 * B * N * KVR * H * (NOPE + VDIM)
 
 
@@ -30,8 +32,7 @@ def tile_multilatentattention_pb_t_kernel(tc, x, Wkva, Wkvb, out_0, out_1):
         outp = ctx.enter_context(tc.tile_pool(name="outp", bufs=3))
         xpp = ctx.enter_context(tc.tile_pool(name="xpp", bufs=2))
         ps_xt = ctx.enter_context(tc.psum_pool(name="ps_xt", bufs=2))
-        ps_mx = ctx.enter_context(tc.psum_pool(name="ps_mx", bufs=4))
-        ps_kv = ctx.enter_context(tc.psum_pool(name="ps_kv", bufs=2))
+        ps_mx = ctx.enter_context(tc.psum_pool(name="ps_mx", bufs=6))
 
         wa_raw = const.tile([P, 2, 4, WA], BF16)
         wb_raw = const.tile([P, 4, 512], BF16)
@@ -176,8 +177,23 @@ def tile_multilatentattention_pb_t_kernel(tc, x, Wkva, Wkvb, out_0, out_1):
                         stop=(g == 1),
                     )
             st[("kp", i)] = kp
-            st[("kf", i)] = outp.tile([P, H, 4, NOPE + ROPE], F32, name="kf")
-            st[("vv", i)] = outp.tile([P, H, 4, VDIM], F32, name="vv")
+            if i < FIRST_HALF:
+                kf = outp.tile([P, H, 4, NOPE + ROPE], F32, name="kf")
+                st[("kf", i)] = kf[:]
+            if i < FIRST_HALF_V:
+                vv = outp.tile([P, H, 4, VDIM], F32, name="vv")
+                st[("vv", i)] = vv[:]
+            for pr in range(2):
+                words = x_sb[2 * max(0, i - FIRST_HALF) + pr][:].rearrange("p t k -> p (t k)").bitcast(F32)
+                cut = H * 2 * (NOPE + ROPE)
+                if i < FIRST_HALF:
+                    st[("kf", i, pr)] = kf[:, :, 2 * pr : 2 * pr + 2, :]
+                else:
+                    st[("kf", i, pr)] = words[:, :cut].rearrange("p (h t f) -> p h t f", h=H, t=2)
+                if i < FIRST_HALF_V:
+                    st[("vv", i, pr)] = vv[:, :, 2 * pr : 2 * pr + 2, :]
+                else:
+                    st[("vv", i, pr)] = words[:, cut:].rearrange("p (h t f) -> p h t f", h=H, t=2)
 
         def rope_mul(i):
             pt = work.tile([P, 4, 2, 2, 64], F32, name="pt")
@@ -190,20 +206,24 @@ def tile_multilatentattention_pb_t_kernel(tc, x, Wkva, Wkvb, out_0, out_1):
             )
             st[("pt", i)] = pt
 
-        def rope_add(i):
-            pt = st[("pt", i)]
+        def second(i):
+            return (0, 4) if i < FIRST_HALF else (2, 2)
+
+        def rope_add(i, lo=0, n=4):
+            pt = st[("pt", i)][:, lo : lo + n]
+            kf = st[("kf", i)] if n == 4 else st[("kf", i, lo // 2)]
             nc.vector.tensor_tensor(
-                out=st[("kf", i)][:, 0, :, NOPE:].rearrange("p t (c r) -> p t c r", r=2),
+                out=kf[:, 0, :, NOPE:].rearrange("p t (c r) -> p t c r", r=2),
                 in0=pt[:, :, 0, :, :].rearrange("p t r c -> p t c r"),
                 in1=pt[:, :, 1, :, :].rearrange("p t r c -> p t c r"),
                 op=ALU.add,
             )
 
-        def rope_rep(i):
-            kf = st[("kf", i)]
+        def rope_rep(i, lo=0, n=4):
+            kf = st[("kf", i)] if n == 4 else st[("kf", i, lo // 2)]
             nc.vector.tensor_copy(
                 out=kf[:, 1:H, :, NOPE:].rearrange("p h t c -> p t h c"),
-                in_=kf[:, 0, :, NOPE:].unsqueeze(2).to_broadcast([P, 4, H - 1, ROPE]),
+                in_=kf[:, 0, :, NOPE:].unsqueeze(2).to_broadcast([P, n, H - 1, ROPE]),
             )
 
         def latent_mm(i, j):
@@ -238,7 +258,7 @@ def tile_multilatentattention_pb_t_kernel(tc, x, Wkva, Wkvb, out_0, out_1):
 
         def kv_mm(i, pr):
             for s in range(2):
-                bank = ps_kv.tile([P, 2, H, 64], F32, name="kv")
+                bank = ps_mx.tile([P, 2, H, 64], F32, name="mx")
                 st[("kv", i, pr, s)] = bank
                 for jj in range(2):
                     j = 2 * pr + jj
@@ -253,24 +273,16 @@ def tile_multilatentattention_pb_t_kernel(tc, x, Wkva, Wkvb, out_0, out_1):
                     )
 
         def kv_out(i, pr, s, eng):
-            dst = st[("kf", i)][:, :, 2 * pr : 2 * pr + 2, 0:NOPE] if s == 0 else st[("vv", i)][:, :, 2 * pr : 2 * pr + 2, :]
+            dst = st[("kf", i, pr)][:, :, :, 0:NOPE] if s == 0 else st[("vv", i, pr)]
             copy(eng, dst.rearrange("p h j c -> p j h c"), st[("kv", i, pr, s)][:])
 
-        def store_kf(i, lo, n):
-            b = i // 2
-            t0 = 4 * (i % 2) + lo
-            nc.sync.dma_start(
-                out=out_0[b].rearrange("h (p t) f -> p h t f", t=8)[:, :, t0 : t0 + n, :],
-                in_=st[("kf", i)][:, :, lo : lo + n, :],
-            )
-
-        def store_vv(i, lo, n):
-            b = i // 2
-            t0 = 4 * (i % 2) + lo
-            nc.sync.dma_start(
-                out=out_1[b].rearrange("h (p t) f -> p h t f", t=8)[:, :, t0 : t0 + n, :],
-                in_=st[("vv", i)][:, :, lo : lo + n, :],
-            )
+        def store(out, name, i, pr):
+            t0 = 4 * (i % 2)
+            dst = out[i // 2].rearrange("h (p t) f -> p h t f", t=8)
+            if i >= (FIRST_HALF if name == "kf" else FIRST_HALF_V):
+                nc.sync.dma_start(out=dst[:, :, t0 + 2 * pr : t0 + 2 * pr + 2, :], in_=st[(name, i, pr)])
+            elif pr == 1:
+                nc.sync.dma_start(out=dst[:, :, t0 : t0 + 4, :], in_=st[(name, i)])
 
         def quant_b():
             nc.vector.quantize_mx(out=wb_c[:].bitcast(FP8X4), scales=wb_s[:], in_=wb_g[:].rearrange("p w t -> p (w t)"))
@@ -339,7 +351,7 @@ def tile_multilatentattention_pb_t_kernel(tc, x, Wkva, Wkvb, out_0, out_1):
                     cosines(3)
                 latent_mm(n, 1)
             if n >= 1:
-                rope_add(n - 1)
+                rope_add(n - 1, *second(n - 1))
             if n < UNITS:
                 c_out(n, 1, "V")
             if n + 1 < UNITS:
@@ -348,37 +360,44 @@ def tile_multilatentattention_pb_t_kernel(tc, x, Wkva, Wkvb, out_0, out_1):
                 x_out(n + 1, 0, "S")
                 x_out(n + 1, 1, "S")
             if n >= 1:
-                rope_rep(n - 1)
+                rope_rep(n - 1, *second(n - 1))
                 kv_mm(n - 1, 1)
                 kv_out(n - 1, 1, 1, "S")
-                store_vv(n - 1, 0, 4)
+                store(out_1, "vv", n - 1, 1)
                 kv_out(n - 1, 1, 0, "S")
-                store_kf(n - 1, 0, 4)
+                store(out_0, "kf", n - 1, 1)
             if n < UNITS:
                 quant_c(n, 0, 1)
-                rope_mm(n)
-                rope_mul(n)
                 if n == 0:
                     regroup_b("V", 0)
                     regroup_b("V", 1)
                     quant_b()
-            if n + 1 < UNITS:
-                quant_x(n + 1, 0, 1)
-            if (n + 2) % 2 == 1 and 3 <= n + 2 < UNITS:
-                permute(n + 2)
-            if n < UNITS:
                 latent_mm(n, 2)
                 c_out(n, 2, "S")
+                rope_mm(n)
+            if n + 1 < UNITS:
+                quant_x(n + 1, 0, 1)
+            if 3 <= n + 2 < UNITS:
+                permute(n + 2)
+            if n < UNITS:
+                rope_mul(n)
             if n + 1 < UNITS:
                 transposes(n + 1, 2)
                 transposes(n + 1, 3)
                 x_out(n + 1, 2, "S")
-                x_out(n + 1, 3, "V" if n % 2 == 0 else "S")
+                x_out(n + 1, 3, "S")
             if n < UNITS:
                 latent_mm(n, 3)
                 c_out(n, 3, "S")
                 kv_mm(n, 0)
-                kv_out(n, 0, 0, "S")
-                kv_out(n, 0, 1, "S")
+                if n >= FIRST_HALF:
+                    rope_add(n, 0, 2)
             if n + 1 < UNITS:
                 quant_x(n + 1, 1, 1)
+            if n < UNITS:
+                if n >= FIRST_HALF:
+                    rope_rep(n, 0, 2)
+                kv_out(n, 0, 0, "S")
+                store(out_0, "kf", n, 0)
+                kv_out(n, 0, 1, "S")
+                store(out_1, "vv", n, 0)

@@ -342,7 +342,7 @@ def tile_multilatentattention_pb_t_kernel(tc, x, Wkva, Wkvb, out_0, out_1):
         quant_w(1, KVR, WA)
 
         for n in range(UNITS + 1):
-            if n >= 1:
+            if 1 <= n < UNITS:
                 quant_c(n - 1, 1, 1)
             if n < UNITS:
                 latent_mm(n, 0)
@@ -364,7 +364,7 @@ def tile_multilatentattention_pb_t_kernel(tc, x, Wkva, Wkvb, out_0, out_1):
                 kv_mm(n - 1, 1)
                 kv_out(n - 1, 1, 1, "S")
                 store(out_1, "vv", n - 1, 1)
-                kv_out(n - 1, 1, 0, "S")
+                kv_out(n - 1, 1, 0, "S" if n < UNITS else "V")
                 store(out_0, "kf", n - 1, 1)
             if n < UNITS:
                 quant_c(n, 0, 1)
@@ -373,12 +373,15 @@ def tile_multilatentattention_pb_t_kernel(tc, x, Wkva, Wkvb, out_0, out_1):
                     regroup_b("V", 1)
                     quant_b()
                 latent_mm(n, 2)
-                c_out(n, 2, "S")
+                if n in (0, 1, 3, 5, 7):
+                    c_out(n, 2, "S")
                 rope_mm(n)
             if n + 1 < UNITS:
                 quant_x(n + 1, 0, 1)
-            if 3 <= n + 2 < UNITS:
+            if n + 2 in (3, 5, 7):
                 permute(n + 2)
+            elif n in (2, 4, 6):
+                c_out(n, 2, "V")
             if n < UNITS:
                 rope_mul(n)
             if n + 1 < UNITS:
@@ -395,9 +398,10 @@ def tile_multilatentattention_pb_t_kernel(tc, x, Wkva, Wkvb, out_0, out_1):
             if n + 1 < UNITS:
                 quant_x(n + 1, 1, 1)
             if n < UNITS:
+                if n == UNITS - 1:
+                    quant_c(n, 1, 1)
                 if n >= FIRST_HALF:
                     rope_rep(n, 0, 2)
-                kv_out(n, 0, 0, "S")
+                for s in (0, 1) if n < FIRST_HALF else (1, 0):
+                    kv_out(n, 0, s, "S")
                 store(out_0, "kf", n, 0)
-                kv_out(n, 0, 1, "S")
-                store(out_1, "vv", n, 0)

import math
from contextlib import ExitStack

import concourse.mybir as mybir
from concourse.masks import make_identity

F32 = mybir.dt.float32
BF16 = mybir.dt.bfloat16
U32 = mybir.dt.uint32
U8 = mybir.dt.uint8
I32 = mybir.dt.int32
FP8X4 = mybir.dt.float8_e4m3fn_x4
ALU = mybir.AluOpType
ACT = mybir.ActivationFunctionType

P = 128
B, N, E, H, NOPE, VDIM, ROPE, KVR = 4, 1024, 1024, 4, 64, 64, 128, 512
BASE = 10000.0
WA = KVR + ROPE
UNITS = 8
FIRST_HALF = 5
FIRST_HALF_V = 8
FLOPS = 2 * B * N * E * WA + 2 * B * N * KVR * H * (NOPE + VDIM)


def tile_multilatentattention_pb_t_kernel(tc, x, Wkva, Wkvb, out_0, out_1):
    nc = tc.nc
    with ExitStack() as ctx:
        ctx.enter_context(tc.manual_schedule())
        const = ctx.enter_context(tc.tile_pool(name="const", bufs=1))
        work = ctx.enter_context(tc.tile_pool(name="work", bufs=2))
        outp = ctx.enter_context(tc.tile_pool(name="outp", bufs=3))
        xpp = ctx.enter_context(tc.tile_pool(name="xpp", bufs=2))
        ps_xt = ctx.enter_context(tc.psum_pool(name="ps_xt", bufs=2))
        ps_mx = ctx.enter_context(tc.psum_pool(name="ps_mx", bufs=6))

        wa_raw = const.tile([P, 2, 4, WA], BF16)
        wb_raw = const.tile([P, 4, 512], BF16)
        x_sb = []
        for i in range(UNITS):
            x_sb.append(const.tile([P, 4, E], BF16, name="x_sb%d" % i))
        ident = const.tile([P, P], F32)
        n_f = const.tile([P, 8], F32)
        one = const.tile([P, 1], F32)
        junk = const.tile([P, 1], F32)
        half_pi = const.tile([P, 1], F32)
        u_t = const.tile([P, 64], F32)
        t_a = const.tile([P, 8, 64], F32)
        t_b = const.tile([P, 8, 64], F32)
        t_k = const.tile([P, 8, 64], I32)
        cs = const.tile([P, 8, 4, 64], F32)
        wa_g = const.tile([P, 2, WA, 4], BF16, align_bytes=64)
        wa_c = const.tile([P, 2, WA], U32, align_bytes=64)
        wa_s = const.tile([P, 2, WA], U8, align_bytes=64)
        wb_g = const.tile([P, 512, 4], BF16, align_bytes=64)
        wb_c = const.tile([P, 512], U32, align_bytes=64)
        wb_s = const.tile([P, 512], U8, align_bytes=64)
        st = {}

        def copy(eng, out, in_):
            if eng == "S":
                nc.scalar.copy(out=out, in_=in_)
            else:
                nc.vector.tensor_copy(out=out, in_=in_)

        def load_wa(g):
            nc.sync.dma_start(
                out=wa_raw[:, g, :, :],
                in_=Wkva[512 * g : 512 * (g + 1), :].rearrange("(q t) c -> q t c", t=4),
            )

        def load_x(i, lo, n):
            src = x[i // 2].rearrange("(p t) k -> p t k", t=8)
            t0 = 4 * (i % 2) + lo
            nc.sync.dma_start(out=x_sb[i][:, lo : lo + n, :], in_=src[:, t0 : t0 + n, :])

        def tables():
            nc.vector.tensor_scalar_mul(out=u_t[:, 0:1], in0=one[:], scalar1=1.0 / (2.0 * math.pi))
            s = 1
            while s < 64:
                nc.vector.tensor_scalar_mul(out=u_t[:, s : 2 * s], in0=u_t[:, 0:s], scalar1=BASE ** (-2.0 * s / ROPE))
                s *= 2
            nc.vector.tensor_tensor(
                out=t_a[:],
                in0=n_f[:].unsqueeze(2).to_broadcast([P, 8, 64]),
                in1=u_t[:].unsqueeze(1).to_broadcast([P, 8, 64]),
                op=ALU.mult,
            )
            nc.vector.tensor_copy(out=t_k[:], in_=t_a[:])
            nc.vector.tensor_tensor(out=t_a[:], in0=t_a[:], in1=t_k[:], op=ALU.subtract)

        def cosines(k):
            nc.scalar.activation(out=cs[:, :, k, :], in_=t_b[:], func=ACT.Sin, scale=-2.0 * math.pi, bias=half_pi[:])

        def sines(k, sign):
            nc.scalar.activation(out=cs[:, :, k, :], in_=t_a[:], func=ACT.Sin, scale=sign * 2.0 * math.pi)

        def regroup_a(g, eng, lo, hi):
            copy(
                eng,
                wa_g[:, g, 0:KVR, :].rearrange("p (m q) t -> p q t m", m=4)[:, lo:hi],
                wa_raw[:, g, :, 0:KVR].rearrange("p t (q m) -> p q t m", m=4)[:, lo:hi],
            )

        def regroup_r(g, eng):
            copy(
                eng,
                wa_g[:, g, KVR:WA, :].rearrange("p (h i) t -> p h i t", h=2),
                wa_raw[:, g, :, KVR:WA].rearrange("p t (i h) -> p h i t", h=2),
            )

        def quant_w(g, lo, hi):
            nc.vector.quantize_mx(
                out=wa_c[:, g, lo:hi].bitcast(FP8X4),
                scales=wa_s[:, g, lo:hi],
                in_=wa_g[:, g, lo:hi, :].rearrange("p w t -> p (w t)"),
            )

        def regroup_b(eng, s):
            copy(
                eng,
                wb_g[:, 256 * s : 256 * (s + 1), :].rearrange("p (h c) t -> p h c t", h=H),
                wb_raw[:].rearrange("p t (h s c) -> p s h c t", h=H, s=2)[:, s],
            )

        def cols(i, t, g, u):
            if ("xp", i) in st:
                c0 = 256 * g + 128 * u
                return st[("xp", i)][:, t, c0 : c0 + 128]
            return x_sb[i][:, t, :].bitcast(F32)[:, 256 * g + u : 256 * (g + 1) : 2]

        def transposes(i, q):
            pr, g = q // 2, q % 2
            xt = ps_xt.tile([P, 2, 256], F32, name="xt")
            for u in range(2):
                for jj in range(2):
                    nc.tensor.transpose(
                        xt[:, u, 128 * jj : 128 * (jj + 1)],
                        cols(i, 2 * pr + jj, g, u),
                        ident[:],
                    )
            st[("xt", i, q)] = xt
            if q == 0:
                st[("xg", i)] = work.tile([P, 2048], F32, name="xg", align_bytes=64)
                st[("xc", i)] = work.tile([P, 1024], U32, name="xc", align_bytes=64)
                st[("xs", i)] = work.tile([P, 1024], U8, name="xs", align_bytes=64)

        def x_out(i, q, eng):
            copy(
                eng,
                st[("xg", i)][:, 512 * q : 512 * (q + 1)].rearrange("p (r u) -> p r u", u=2),
                st[("xt", i, q)][:].rearrange("p u r -> p r u"),
            )

        def quant_x(i, lo, n):
            nc.vector.quantize_mx(
                out=st[("xc", i)][:, 512 * lo : 512 * (lo + n)].bitcast(FP8X4),
                scales=st[("xs", i)][:, 512 * lo : 512 * (lo + n)],
                in_=st[("xg", i)][:, 1024 * lo : 1024 * (lo + n)].bitcast(BF16),
            )

        def x_cols(j, g):
            c0 = ((j // 2) * 2 + g) * 256 + (j % 2) * 128
            return slice(c0, c0 + 128)

        def rope_mm(i):
            kp = ps_mx.tile([P, 4, 128], F32, name="mx")
            for j in range(4):
                for g in range(2):
                    nc.tensor.matmul_mx(
                        out=kp[:, j, :],
                        lhsT=st[("xc", i)][:, x_cols(j, g)].bitcast(FP8X4),
                        lhsT_scale=st[("xs", i)][:, x_cols(j, g)],
                        rhs=wa_c[:, g, KVR:WA].bitcast(FP8X4),
                        rhs_scale=wa_s[:, g, KVR:WA],
                        start=(g == 0),
                        stop=(g == 1),
                    )
            st[("kp", i)] = kp
            if i < FIRST_HALF:
                kf = outp.tile([P, H, 4, NOPE + ROPE], F32, name="kf")
                st[("kf", i)] = kf[:]
            if i < FIRST_HALF_V:
                vv = outp.tile([P, H, 4, VDIM], F32, name="vv")
                st[("vv", i)] = vv[:]
            for pr in range(2):
                words = x_sb[2 * max(0, i - FIRST_HALF) + pr][:].rearrange("p t k -> p (t k)").bitcast(F32)
                cut = H * 2 * (NOPE + ROPE)
                if i < FIRST_HALF:
                    st[("kf", i, pr)] = kf[:, :, 2 * pr : 2 * pr + 2, :]
                else:
                    st[("kf", i, pr)] = words[:, :cut].rearrange("p (h t f) -> p h t f", h=H, t=2)
                if i < FIRST_HALF_V:
                    st[("vv", i, pr)] = vv[:, :, 2 * pr : 2 * pr + 2, :]
                else:
                    st[("vv", i, pr)] = words[:, cut:].rearrange("p (h t f) -> p h t f", h=H, t=2)

        def rope_mul(i):
            pt = work.tile([P, 4, 2, 2, 64], F32, name="pt")
            t0 = 4 * (i % 2)
            nc.vector.tensor_tensor(
                out=pt[:].rearrange("p t h r c -> p (t h) r c"),
                in0=st[("kp", i)][:].rearrange("p t (h c) -> p (t h) c", h=2).unsqueeze(2).to_broadcast([P, 8, 2, 64]),
                in1=cs[:, t0 : t0 + 4, :, :].rearrange("p t (h r) c -> p (t h) r c", h=2),
                op=ALU.mult,
            )
            st[("pt", i)] = pt

        def second(i):
            return (0, 4) if i < FIRST_HALF else (2, 2)

        def rope_add(i, lo=0, n=4):
            pt = st[("pt", i)][:, lo : lo + n]
            kf = st[("kf", i)] if n == 4 else st[("kf", i, lo // 2)]
            nc.vector.tensor_tensor(
                out=kf[:, 0, :, NOPE:].rearrange("p t (c r) -> p t c r", r=2),
                in0=pt[:, :, 0, :, :].rearrange("p t r c -> p t c r"),
                in1=pt[:, :, 1, :, :].rearrange("p t r c -> p t c r"),
                op=ALU.add,
            )

        def rope_rep(i, lo=0, n=4):
            kf = st[("kf", i)] if n == 4 else st[("kf", i, lo // 2)]
            nc.vector.tensor_copy(
                out=kf[:, 1:H, :, NOPE:].rearrange("p h t c -> p t h c"),
                in_=kf[:, 0, :, NOPE:].unsqueeze(2).to_broadcast([P, n, H - 1, ROPE]),
            )

        def latent_mm(i, j):
            ct = ps_mx.tile([P, 4, 128], F32, name="mx")
            for m in range(4):
                for g in range(2):
                    nc.tensor.matmul_mx(
                        out=ct[:, m, :],
                        lhsT=wa_c[:, g, 128 * m : 128 * (m + 1)].bitcast(FP8X4),
                        lhsT_scale=wa_s[:, g, 128 * m : 128 * (m + 1)],
                        rhs=st[("xc", i)][:, x_cols(j, g)].bitcast(FP8X4),
                        rhs_scale=st[("xs", i)][:, x_cols(j, g)],
                        start=(g == 0),
                        stop=(g == 1),
                    )
            st[("ct", i, j)] = ct
            if j == 0:
                st[("cg", i)] = work.tile([P, 512, 4], BF16, name="cg", align_bytes=64)

        def c_out(i, j, eng):
            copy(eng, st[("cg", i)][:, 128 * j : 128 * (j + 1), :], st[("ct", i, j)][:].rearrange("p m r -> p r m"))

        def quant_c(i, lo, n):
            if lo == 0:
                st[("cc", i)] = work.tile([P, 512], U32, name="cc", align_bytes=64)
                st[("cs", i)] = work.tile([P, 512], U8, name="csc", align_bytes=64)
            nc.vector.quantize_mx(
                out=st[("cc", i)][:, 256 * lo : 256 * (lo + n)].bitcast(FP8X4),
                scales=st[("cs", i)][:, 256 * lo : 256 * (lo + n)],
                in_=st[("cg", i)][:, 256 * lo : 256 * (lo + n), :].rearrange("p w t -> p (w t)"),
            )

        def kv_mm(i, pr):
            for s in range(2):
                bank = ps_mx.tile([P, 2, H, 64], F32, name="mx")
                st[("kv", i, pr, s)] = bank
                for jj in range(2):
                    j = 2 * pr + jj
                    nc.tensor.matmul_mx(
                        out=bank[:, jj, :, :].rearrange("p h c -> p (h c)"),
                        lhsT=st[("cc", i)][:, 128 * j : 128 * (j + 1)].bitcast(FP8X4),
                        lhsT_scale=st[("cs", i)][:, 128 * j : 128 * (j + 1)],
                        rhs=wb_c[:, 256 * s : 256 * (s + 1)].bitcast(FP8X4),
                        rhs_scale=wb_s[:, 256 * s : 256 * (s + 1)],
                        start=True,
                        stop=True,
                    )

        def kv_out(i, pr, s, eng):
            dst = st[("kf", i, pr)][:, :, :, 0:NOPE] if s == 0 else st[("vv", i, pr)]
            copy(eng, dst.rearrange("p h j c -> p j h c"), st[("kv", i, pr, s)][:])

        def store(out, name, i, pr):
            t0 = 4 * (i % 2)
            dst = out[i // 2].rearrange("h (p t) f -> p h t f", t=8)
            if i >= (FIRST_HALF if name == "kf" else FIRST_HALF_V):
                nc.sync.dma_start(out=dst[:, :, t0 + 2 * pr : t0 + 2 * pr + 2, :], in_=st[(name, i, pr)])
            elif pr == 1:
                nc.sync.dma_start(out=dst[:, :, t0 : t0 + 4, :], in_=st[(name, i)])

        def quant_b():
            nc.vector.quantize_mx(out=wb_c[:].bitcast(FP8X4), scales=wb_s[:], in_=wb_g[:].rearrange("p w t -> p (w t)"))

        def load_b():
            nc.sync.dma_start(out=wb_raw[:], in_=Wkvb.rearrange("(p t) n -> p t n", t=4))

        def consts():
            nc.vector.memset(one[:], 1.0)
            nc.gpsimd.iota(out=n_f[:], pattern=[[1, 8]], base=0, channel_multiplier=8, allow_small_or_imprecise_dtypes=True)
            make_identity(nc, ident[:])
            nc.scalar.activation(out=junk[:], in_=one[:], func=ACT.Sin)
            nc.scalar.mul(out=half_pi[:], in_=one[:], mul=math.pi / 2.0)

        def absf():
            nc.scalar.activation(out=t_b[:], in_=t_a[:], func=ACT.Abs)

        def permute(i):
            st[("xp", i)] = xpp.tile([P, 4, 512], F32, name="xp")
            nc.vector.tensor_copy(
                out=st[("xp", i)][:].rearrange("p t (g u w) -> p (t g) u w", g=2, u=2),
                in_=x_sb[i][:].bitcast(F32).rearrange("p t (g w u) -> p (t g) u w", g=2, u=2),
            )

        load_wa(0)
        load_x(0, 0, 2)
        load_wa(1)
        load_x(0, 2, 2)
        load_x(1, 0, 4)
        load_b()
        for i in range(2, UNITS):
            load_x(i, 0, 4)
        consts()
        tables()
        absf()
        cosines(0)
        regroup_a(0, "V", 0, 128)
        transposes(0, 0)
        transposes(0, 1)
        x_out(0, 0, "S")
        x_out(0, 1, "S")
        quant_w(0, 0, KVR)
        regroup_a(1, "V", 0, 96)
        regroup_a(1, "S", 96, 128)
        quant_x(0, 0, 1)
        quant_w(1, 0, KVR)
        transposes(0, 2)
        transposes(0, 3)
        sines(1, 1.0)
        x_out(0, 2, "S")
        x_out(0, 3, "S")
        regroup_r(0, "V")
        regroup_r(1, "V")
        sines(2, -1.0)
        quant_x(0, 1, 1)
        quant_w(0, KVR, WA)
        quant_w(1, KVR, WA)

        for n in range(UNITS + 1):
            if 1 <= n < UNITS:
                quant_c(n - 1, 1, 1)
            if n < UNITS:
                latent_mm(n, 0)
                c_out(n, 0, "S")
                if n == 0:
                    cosines(3)
                latent_mm(n, 1)
            if n >= 1:
                rope_add(n - 1, *second(n - 1))
            if n < UNITS:
                c_out(n, 1, "V")
            if n + 1 < UNITS:
                transposes(n + 1, 0)
                transposes(n + 1, 1)
                x_out(n + 1, 0, "S")
                x_out(n + 1, 1, "S")
            if n >= 1:
                rope_rep(n - 1, *second(n - 1))
                kv_mm(n - 1, 1)
                kv_out(n - 1, 1, 1, "S")
                store(out_1, "vv", n - 1, 1)
                kv_out(n - 1, 1, 0, "S" if n < UNITS else "V")
                store(out_0, "kf", n - 1, 1)
            if n < UNITS:
                quant_c(n, 0, 1)
                if n == 0:
                    regroup_b("V", 0)
                    regroup_b("V", 1)
                    quant_b()
                latent_mm(n, 2)
                if n in (0, 1, 3, 5, 7):
                    c_out(n, 2, "S")
                rope_mm(n)
            if n + 1 < UNITS:
                quant_x(n + 1, 0, 1)
            if n + 2 in (3, 5, 7):
                permute(n + 2)
            elif n in (2, 4, 6):
                c_out(n, 2, "V")
            if n < UNITS:
                rope_mul(n)
            if n + 1 < UNITS:
                transposes(n + 1, 2)
                transposes(n + 1, 3)
                x_out(n + 1, 2, "S")
                x_out(n + 1, 3, "S")
            if n < UNITS:
                latent_mm(n, 3)
                c_out(n, 3, "S")
                kv_mm(n, 0)
                if n >= FIRST_HALF:
                    rope_add(n, 0, 2)
            if n + 1 < UNITS:
                quant_x(n + 1, 1, 1)
            if n < UNITS:
                if n == UNITS - 1:
                    quant_c(n, 1, 1)
                if n >= FIRST_HALF:
                    rope_rep(n, 0, 2)
                for s in (0, 1) if n < FIRST_HALF else (1, 0):
                    kv_out(n, 0, s, "S")
                store(out_0, "kf", n, 0)
